import numpy as np
import ml_dtypes


def mxq(x, axis, fmt="e4m3"):
    dtype, down = {"e4m3": (ml_dtypes.float8_e4m3fn, 7), "e5m2": (ml_dtypes.float8_e5m2, 14)}[fmt]
    v = np.moveaxis(np.asarray(x, np.float32).astype(ml_dtypes.bfloat16).astype(np.float64), axis, -1)
    blocks = v.reshape(v.shape[:-1] + (-1, 32))
    amax = np.abs(blocks).max(-1, keepdims=True)
    byte = np.maximum(np.where(amax > 0, np.frexp(amax)[1] - 1 + 127, 0) - down, 1)
    scale = np.exp2(byte - 127.0)
    codes = (blocks / scale).astype(np.float32).astype(dtype).astype(np.float64)
    return np.moveaxis((codes * scale).reshape(v.shape), -1, axis)


WIDE = False


def mx_kscale(k):
    if not WIDE:
        return np.ones(k)
    levels = np.array([10, -10, 5, -5, 0])
    a = np.random.permutation(np.resize(levels, k // 512 * 4)).reshape(k // 512, 4)
    idx = np.arange(k)
    return np.exp2(a[idx // 512, idx % 128 // 32])


BF16 = ml_dtypes.bfloat16


def bf(x):
    return np.asarray(x, np.float32).astype(BF16)


def f64(x):
    return np.asarray(x).astype(np.float64)


B, STOCH, ACT_DIM, HIDDEN, DETER = 4096, 1024, 512, 2048, 512
EPS = 1e-4
DT_MIN = 1e-4


def softplus(v):
    return np.maximum(v, 0.0) + np.log1p(np.exp(-np.abs(v)))


def sigmoid(v):
    return 1.0 / (1.0 + np.exp(-v))


def rmsnorm(v, w):
    return v * (1.0 / np.sqrt(np.mean(v * v, axis=-1, keepdims=True) + EPS)) * w


def setup_inputs():
    s = mx_kscale(DETER)
    r = np.maximum(s, 1.0)

    def w():
        return np.random.standard_normal((DETER, DETER)) / np.sqrt(DETER) / s

    def bias():
        return np.random.standard_normal(DETER) * 0.2

    return {"x": bf(np.random.standard_normal((B, DETER)) * 0.9 * s),
            "deter": bf(np.random.standard_normal((B, DETER))),
            "a_base": bf(np.random.standard_normal(DETER)),
            "dt_w": bf(w()), "dt_b": bf(bias()),
            "b_w": bf(w()), "b_b": bf(bias()),
            "c_w": bf(w() / r[:, None]), "c_b": bf(bias() / r),
            "z_w": bf(w()), "z_b": bf(bias()),
            "skip": bf(np.random.standard_normal(DETER) * 0.5 / s),
            "norm_w": bf(1.0 + 0.1 * np.random.standard_normal(DETER))}


def reference(x, deter, a_base, dt_w, dt_b, b_w, b_b, c_w, c_b, z_w, z_b, skip, norm_w):
    x, deter = f64(x), f64(deter)
    xq = mxq(x, 1, "e4m3")
    dt = softplus((xq @ mxq(f64(dt_w), 1, "e4m3").T) + f64(dt_b)) + DT_MIN
    a = -softplus(f64(a_base))
    b = np.tanh((xq @ mxq(f64(b_w), 1, "e4m3").T) + f64(b_b))
    c = (xq @ mxq(f64(c_w), 1, "e4m3").T) + f64(c_b)
    z = sigmoid((xq @ mxq(f64(z_w), 1, "e4m3").T) + f64(z_b))
    state = np.exp(a * dt) * deter + dt * b * x
    y = c * state + f64(skip) * x
    out = z * y + (1.0 - z) * deter
    return rmsnorm(out, f64(norm_w))

@@ -1,0 +1,420 @@
+from contextlib import ExitStack
+
+import concourse.mybir as mybir
+from concourse.masks import make_identity
+
+F32 = mybir.dt.float32
+BF16 = mybir.dt.bfloat16
+U32 = mybir.dt.uint32
+U8 = mybir.dt.uint8
+FP8X4 = mybir.dt.float8_e4m3fn_x4
+FUNC = mybir.ActivationFunctionType
+ALU = mybir.AluOpType
+
+P = 128
+PACK = 4
+TOKENS = 4096
+CHANNELS = 512
+GROUP = 512
+ROWS = GROUP // P
+N_GROUPS = TOKENS // GROUP
+CH_TILES = CHANNELS // P
+N_BLOCKS = N_GROUPS * CH_TILES
+ROUND = 8
+AHEAD = 2
+NORM_LAG = 5
+NATURAL_BUFS = 6
+DT_MIN = 1e-4
+EXP_DT_MIN_LESS_1 = DT_MIN + DT_MIN**2 / 2 + DT_MIN**3 / 6
+EXP_CAP = 2.0**60
+EPS = 1e-4
+
+W_DT, W_B, W_C, W_Z = 0, 1, 2, 3
+N_WEIGHTS = 4
+V_A, V_DT_B, V_B_B, V_C_B, V_Z_B, V_SKIP = 0, 1, 2, 3, 4, 5
+N_VECTORS = 6
+
+FLOPS = 4 * 2 * TOKENS * CHANNELS * CHANNELS
+
+
+def tile_mamba2backbone_pb_t_kernel(
+    tc, x, deter, a_base, dt_w, dt_b, b_w, b_b, c_w, c_b, z_w, z_b, skip, norm_w, out
+):
+    nc = tc.nc
+    x_groups = x.rearrange("(g p r) c -> g p r c", p=P, r=ROWS)
+    deter_groups = deter.rearrange("(g p r) c -> g p r c", p=P, r=ROWS)
+    out_groups = out.rearrange("(g p r) c -> g p r c", p=P, r=ROWS)
+
+    with ExitStack() as stack:
+        keep = stack.enter_context(tc.tile_pool(name="keep", bufs=1))
+        natural = stack.enter_context(tc.tile_pool(name="natural", bufs=NATURAL_BUFS))
+        regroup = stack.enter_context(tc.tile_pool(name="regroup", bufs=3))
+        work = stack.enter_context(tc.tile_pool(name="work", bufs=3))
+        stats = stack.enter_context(tc.tile_pool(name="stats", bufs=3))
+        dt_pool = stack.enter_context(tc.tile_pool(name="dt_pool", bufs=ROUND + ROUND // 2))
+        gates = stack.enter_context(tc.tile_pool(name="gates", bufs=ROUND + 1))
+        sums = stack.enter_context(tc.tile_pool(name="sums", bufs=CH_TILES + NORM_LAG))
+        psum = stack.enter_context(tc.psum_pool(name="psum", bufs=2))
+        psum_turned = stack.enter_context(tc.psum_pool(name="psum_turned", bufs=4))
+        stack.enter_context(tc.manual_schedule())
+
+        vec_rows = keep.tile([P, P], BF16, name="vec_rows", tag="vec_rows")
+        nc.vector.memset(vec_rows[:], 0.0)
+        one_col = keep.tile([P, 1], F32, name="one_col", tag="one_col")
+        nc.vector.memset(one_col[:], 1.0)
+        neg_half = keep.tile([P, 1], F32, name="neg_half", tag="neg_half")
+        nc.vector.memset(neg_half[:], -0.5)
+        ident_bf = keep.tile([P, P], BF16, name="ident_bf", tag="ident_bf")
+        make_identity(nc, ident_bf[:])
+        ident_f32 = keep.tile([P, P], F32, name="ident_f32", tag="ident_f32")
+        make_identity(nc, ident_f32[:])
+        two_ident = keep.tile([P, P], BF16, name="two_ident", tag="two_ident")
+        nc.vector.tensor_scalar(out=two_ident[:], in0=ident_bf[:], scalar1=2.0, scalar2=None, op0=ALU.mult)
+        exp_dt_min = keep.tile([P, 1], F32, name="exp_dt_min", tag="exp_dt_min")
+        nc.vector.tensor_scalar(out=exp_dt_min[:], in0=one_col[:], scalar1=EXP_DT_MIN_LESS_1, scalar2=None, op0=ALU.add)
+
+        vectors = (a_base, dt_b, b_b, c_b, z_b, skip)
+        for v in range(N_VECTORS):
+            nc.sync.dma_start(
+                out=vec_rows[CH_TILES * v : CH_TILES * (v + 1), :],
+                in_=vectors[v].rearrange("(t p) -> t p", p=P),
+            )
+
+        def load_weight(w):
+            rows = natural.tile([P, ROWS, CHANNELS], BF16, name="rows", tag="rows")
+            nc.sync.dma_start(out=rows[:], in_=w.rearrange("(t p) k -> p t k", p=P))
+            return rows
+
+        def load_x(g):
+            rows = keep.tile([P, ROWS, CHANNELS], BF16, name="x_rows%d" % g, tag="x_rows%d" % g)
+            nc.sync.dma_start(out=rows[:], in_=x_groups[g])
+            return rows
+
+        def load_deter(g):
+            if g < N_GROUPS:
+                deter_rows[g] = natural.tile([P, ROWS, CHANNELS], BF16, name="rows", tag="rows")
+                nc.sync.dma_start(out=deter_rows[g][:], in_=deter_groups[g])
+
+        x_rows = {}
+        deter_rows = {}
+        w_rows = {}
+        w_rows[W_DT] = load_weight(dt_w)
+        x_rows[0] = load_x(0)
+        x_rows[1] = load_x(1)
+        w_rows[W_B] = load_weight(b_w)
+        w_rows[W_Z] = load_weight(z_w)
+        w_rows[W_C] = load_weight(c_w)
+        x_rows[2] = load_x(2)
+        x_rows[3] = load_x(3)
+        load_deter(0)
+        load_deter(1)
+        for g in range(4, N_GROUPS):
+            x_rows[g] = load_x(g)
+        gain = keep.tile([P, CHANNELS], BF16, name="gain", tag="gain")
+        nc.sync.dma_start(out=gain[:], in_=norm_w.partition_broadcast(P))
+        half_gain = keep.tile([P, CHANNELS], BF16, name="half_gain", tag="half_gain")
+
+        turned_vec = psum_turned.tile([P, P], BF16, name="turned_vec", tag="turned")
+        nc.tensor.transpose(turned_vec[:], vec_rows[:], ident_bf[:])
+        cols = keep.tile([P, N_VECTORS, CH_TILES], F32, name="cols", tag="cols")
+        nc.vector.tensor_copy(
+            out=cols[:].rearrange("p v t -> p (v t)"), in_=turned_vec[:, : N_VECTORS * CH_TILES]
+        )
+        dt_b_min = keep.tile([P, CH_TILES], F32, name="dt_b_min", tag="dt_b_min")
+        nc.vector.tensor_scalar(
+            out=dt_b_min[:], in0=cols[:, V_DT_B, :], scalar1=DT_MIN, scalar2=None, op0=ALU.add
+        )
+        half_z_b = keep.tile([P, CH_TILES], F32, name="half_z_b", tag="half_z_b")
+        nc.vector.tensor_scalar(
+            out=half_z_b[:], in0=cols[:, V_Z_B, :], scalar1=0.5, scalar2=None, op0=ALU.mult
+        )
+        neg_relu_a = keep.tile([P, CH_TILES], F32, name="neg_relu_a", tag="neg_relu_a")
+        nc.vector.tensor_scalar(
+            out=neg_relu_a[:], in0=cols[:, V_A, :], scalar1=0.0, scalar2=-1.0, op0=ALU.max, op1=ALU.mult
+        )
+        log_a = keep.tile([P, CH_TILES], F32, name="log_a", tag="log_a")
+        nc.scalar.activation(out=log_a[:], in_=cols[:, V_A, :], func=FUNC.Abs)
+        nc.scalar.activation(out=log_a[:], in_=log_a[:], func=FUNC.Exp, scale=-1.0)
+
+        x_codes = keep.tile([P, N_GROUPS, GROUP], U32, name="x_codes", tag="x_codes", align_bytes=64)
+        x_scales = keep.tile([P, N_GROUPS, GROUP], U8, name="x_scales", tag="x_scales", align_bytes=64)
+        w_codes = keep.tile([P, N_WEIGHTS, CHANNELS], U32, name="w_codes", tag="w_codes", align_bytes=64)
+        w_scales = keep.tile([P, N_WEIGHTS, CHANNELS], U8, name="w_scales", tag="w_scales", align_bytes=64)
+
+        def turn_rows(rows):
+            words = rows[:].bitcast(F32)
+            grouped = regroup.tile([P, ROWS * P * PACK], BF16, name="grouped", tag="grouped", align_bytes=64)
+            grouped_words = grouped[:].bitcast(F32).rearrange("p (n u) -> p n u", u=2)
+            for half in range(2):
+                turned = psum_turned.tile([P, 2, 2 * P], F32, name="turned", tag="turned")
+                for u in range(2):
+                    for j in range(2):
+                        nc.tensor.transpose(
+                            turned[:, u, j * P : (j + 1) * P],
+                            words[:, 2 * half + j, u * P : (u + 1) * P],
+                            ident_f32[:],
+                        )
+                nc.vector.tensor_copy(
+                    out=grouped_words[:, half * 2 * P : (half + 1) * 2 * P, :],
+                    in_=turned[:].rearrange("p u n -> p n u"),
+                )
+            return grouped
+
+        def quantise(grouped, codes, scales):
+            nc.vector.quantize_mx(out=codes.bitcast(FP8X4), scales=scales, in_=grouped[:])
+
+        def quantise_all(jobs):
+            waiting = None
+            for rows, codes, scales in jobs:
+                grouped = turn_rows(rows)
+                if waiting is not None:
+                    quantise(*waiting)
+                waiting = (grouped, codes, scales)
+            quantise(*waiting)
+
+        def weight_job(w):
+            return (w_rows[w], w_codes[:, w, :], w_scales[:, w, :])
+
+        def x_job(g):
+            return (x_rows[g], x_codes[:, g, :], x_scales[:, g, :])
+
+        def is_block(i):
+            return 0 <= i < N_BLOCKS
+
+        def project(w, i, pool, tag):
+            g, t = divmod(i, CH_TILES)
+            acc = pool.tile([P, GROUP], F32, name=tag, tag=tag)
+            nc.tensor.matmul_mx(
+                out=acc[:],
+                lhsT=w_codes[:, w, t * P : (t + 1) * P].bitcast(FP8X4),
+                lhsT_scale=w_scales[:, w, t * P : (t + 1) * P],
+                rhs=x_codes[:, g, :].bitcast(FP8X4),
+                rhs_scale=x_scales[:, g, :],
+                start=True,
+                stop=True,
+            )
+            return acc
+
+        dt = {}
+        decay = {}
+        b_gate = {}
+        z_tanh = {}
+        c_acc = {}
+        turned_xd = {}
+        left = {}
+        right = {}
+        both = {}
+        gated = {}
+
+        def exp_stage(i):
+            if is_block(i):
+                acc = project(W_DT, i, psum, "for_scalar")
+                dt[i] = dt_pool.tile([P, GROUP], F32, name="dt", tag="dt")
+                nc.scalar.activation(
+                    out=dt[i][:], in_=acc[:], func=FUNC.Exp, bias=cols[:, V_DT_B, i % CH_TILES : i % CH_TILES + 1]
+                )
+
+        def clamp_stage(i):
+            if is_block(i):
+                nc.vector.tensor_scalar(out=dt[i][:], in0=dt[i][:], scalar1=EXP_CAP, scalar2=None, op0=ALU.min)
+
+        def ln_stage(i):
+            if is_block(i):
+                nc.scalar.activation(out=dt[i][:], in_=dt[i][:], func=FUNC.Ln, scale=exp_dt_min[:], bias=exp_dt_min[:])
+
+        def large_stage(i):
+            if is_block(i):
+                t = i % CH_TILES
+                acc = project(W_DT, i, psum, "for_scalar")
+                nc.vector.scalar_tensor_tensor(
+                    out=dt[i][:], in0=acc[:], scalar=dt_b_min[:, t : t + 1], in1=dt[i][:], op0=ALU.add, op1=ALU.max
+                )
+
+        def gate_stage(i):
+            if is_block(i):
+                t = i % CH_TILES
+                acc_b = project(W_B, i, psum, "for_scalar")
+                acc_z = project(W_Z, i, psum, "for_scalar")
+                decay[i] = gates.tile([P, GROUP], F32, name="decay", tag="decay")
+                nc.scalar.activation(
+                    out=decay[i][:], in_=dt[i][:], func=FUNC.Exp, scale=a_col[:, t : t + 1]
+                )
+                b_gate[i] = gates.tile([P, GROUP], F32, name="b_gate", tag="b_gate")
+                nc.scalar.activation(out=b_gate[i][:], in_=acc_b[:], func=FUNC.Tanh, bias=cols[:, V_B_B, t : t + 1])
+                z_tanh[i] = gates.tile([P, GROUP], F32, name="z_tanh", tag="z_tanh")
+                nc.scalar.activation(
+                    out=z_tanh[i][:], in_=acc_z[:], func=FUNC.Tanh, scale=0.5, bias=half_z_b[:, t : t + 1]
+                )
+
+        def feed_stage(i):
+            if is_block(i):
+                g, t = divmod(i, CH_TILES)
+                c_acc[i] = project(W_C, i, psum_turned, "turned")
+                turned_xd[i] = psum.tile([P, 2, GROUP], BF16, name="turned_xd", tag="turned_xd")
+                for side, rows in enumerate((x_rows[g], deter_rows[g])):
+                    for r in range(ROWS):
+                        nc.tensor.transpose(
+                            turned_xd[i][:, side, r * P : (r + 1) * P], rows[:, r, t * P : (t + 1) * P], ident_bf[:]
+                        )
+
+        def dt_times_b(i):
+            if is_block(i):
+                right[i] = work.tile([P, GROUP], F32, name="right", tag="right")
+                nc.gpsimd.tensor_tensor(out=right[i][:], in0=dt[i][:], in1=b_gate[i][:], op=ALU.mult)
+
+        def c_times_decay(i):
+            if is_block(i):
+                t = i % CH_TILES
+                left[i] = work.tile([P, GROUP], F32, name="left", tag="left")
+                nc.vector.scalar_tensor_tensor(
+                    out=left[i][:], in0=c_acc[i][:], scalar=cols[:, V_C_B, t : t + 1], in1=decay[i][:],
+                    op0=ALU.add, op1=ALU.mult,
+                )
+
+        def c_times_right(i):
+            if is_block(i):
+                t = i % CH_TILES
+                nc.vector.scalar_tensor_tensor(
+                    out=right[i][:], in0=c_acc[i][:], scalar=cols[:, V_C_B, t : t + 1], in1=right[i][:],
+                    op0=ALU.add, op1=ALU.mult,
+                )
+
+        def left_times_deter(i):
+            if is_block(i):
+                nc.vector.scalar_tensor_tensor(
+                    out=left[i][:], in0=left[i][:], scalar=-1.0, in1=turned_xd[i][:, 1, :], op0=ALU.add, op1=ALU.mult
+                )
+
+        def right_times_x(i):
+            if is_block(i):
+                t = i % CH_TILES
+                nc.vector.scalar_tensor_tensor(
+                    out=right[i][:], in0=right[i][:], scalar=cols[:, V_SKIP, t : t + 1], in1=turned_xd[i][:, 0, :],
+                    op0=ALU.add, op1=ALU.mult,
+                )
+
+        def add_sides(i):
+            if is_block(i):
+                both[i] = work.tile([P, GROUP], F32, name="both", tag="both")
+                nc.gpsimd.tensor_tensor(out=both[i][:], in0=left[i][:], in1=right[i][:], op=ALU.add)
+
+        def times_tanh(i):
+            if is_block(i):
+                gated[i] = sums.tile([P, GROUP], F32, name="gated", tag="gated")
+                nc.vector.scalar_tensor_tensor(
+                    out=gated[i][:], in0=z_tanh[i][:], scalar=1.0, in1=both[i][:], op0=ALU.add, op1=ALU.mult
+                )
+
+        o_turned = {}
+        sum_sq = {}
+        mean_sq = {}
+        rstd = {}
+
+        def turn_back(n):
+            if is_block(n):
+                g, r = divmod(n, ROWS)
+                o_turned[n] = psum_turned.tile([P, CHANNELS], F32, name="turned", tag="turned")
+                nc.tensor.matmul(
+                    out=o_turned[n][:], lhsT=two_ident[:], rhs=deter_rows[g][:, r, :], start=True, stop=False
+                )
+                for t in range(CH_TILES):
+                    nc.tensor.matmul(
+                        out=o_turned[n][:, t * P : (t + 1) * P],
+                        lhsT=gated[CH_TILES * g + t][:, r * P : (r + 1) * P],
+                        rhs=ident_f32[:],
+                        is_transpose=True,
+                        start=False,
+                        stop=(t == CH_TILES - 1),
+                    )
+                squares = work.tile([P, CHANNELS], BF16, name="squares", tag="squares")
+                sum_sq[n] = stats.tile([P, 1], F32, name="sum_sq", tag="sum_sq")
+                nc.scalar.activation(out=squares[:], in_=o_turned[n][:], func=FUNC.Square, accum_out=sum_sq[n][:])
+                if r == ROWS - 1:
+                    load_deter(g + NATURAL_BUFS)
+
+        def mean_stage(n):
+            if is_block(n):
+                mean_sq[n] = stats.tile([P, 1], F32, name="mean_sq", tag="mean_sq")
+                nc.vector.tensor_scalar(
+                    out=mean_sq[n][:], in0=sum_sq[n][:], scalar1=0.25 / CHANNELS, scalar2=EPS, op0=ALU.mult, op1=ALU.add
+                )
+
+        def rstd_stage(n):
+            if is_block(n):
+                rstd[n] = stats.tile([P, 1], F32, name="rstd", tag="rstd")
+                nc.gpsimd.tensor_tensor(out=rstd[n][:], in0=mean_sq[n][:], in1=neg_half[:], op=ALU.pow)
+
+        def scale_and_store(n):
+            if is_block(n):
+                g, r = divmod(n, ROWS)
+                result = work.tile([P, CHANNELS], F32, name="result", tag="result")
+                nc.vector.scalar_tensor_tensor(
+                    out=result[:], in0=o_turned[n][:], scalar=rstd[n][:], in1=half_gain[:], op0=ALU.mult, op1=ALU.mult
+                )
+                nc.sync.dma_start(out=out_groups[g, :, r, :], in_=result[:])
+
+        quantise_all([weight_job(W_DT), x_job(0)])
+        exp_stage(0)
+        exp_stage(1)
+        quantise_all([x_job(1)])
+        for i in range(2, ROUND):
+            exp_stage(i)
+        quantise_all([weight_job(W_B)])
+        for i in range(ROUND // 2):
+            clamp_stage(i)
+        quantise_all([weight_job(W_Z)])
+        for i in range(ROUND // 2, ROUND):
+            clamp_stage(i)
+        nc.scalar.activation(out=log_a[:], in_=log_a[:], func=FUNC.Ln, bias=one_col[:])
+        a_col = keep.tile([P, CH_TILES], F32, name="a_col", tag="a_col")
+        nc.gpsimd.tensor_tensor(out=a_col[:], in0=neg_relu_a[:], in1=log_a[:], op=ALU.subtract)
+        for i in range(ROUND):
+            ln_stage(i)
+        quantise_all([weight_job(W_C)])
+        for i in range(ROUND // 2):
+            large_stage(i)
+        quantise_all([x_job(2)])
+        for i in range(ROUND // 2, ROUND):
+            large_stage(i)
+        quantise_all([x_job(g) for g in range(3, N_GROUPS)])
+        for g in range(2, NATURAL_BUFS):
+            load_deter(g)
+        nc.vector.tensor_scalar(out=half_gain[:], in0=gain[:], scalar1=0.5, scalar2=None, op0=ALU.mult)
+
+        def scalar_stage(step, half):
+            this_round, s = divmod(step + AHEAD, ROUND)
+            if s < ROUND // 2:
+                gate_stage(ROUND * this_round + 2 * s + half)
+            else:
+                for j in range(2):
+                    i = ROUND * (this_round + 1) + (ROUND // 2) * (s % 2) + 2 * half + j
+                    if s < ROUND // 2 + 2:
+                        exp_stage(i)
+                    else:
+                        ln_stage(i)
+
+        def finish_softplus(step):
+            this_round, s = divmod(step + AHEAD, ROUND)
+            for j in range(ROUND // 2):
+                i = ROUND * (this_round + 1) + (ROUND // 2) * (s % 2) + j
+                if ROUND // 2 <= s < ROUND // 2 + 2:
+                    clamp_stage(i)
+                elif s >= ROUND // 2 + 2:
+                    large_stage(i)
+
+        for step in range(-AHEAD, N_BLOCKS + NORM_LAG + 2):
+            feed_stage(step + 1)
+            scalar_stage(step, 0)
+            turn_back(step - NORM_LAG)
+            scalar_stage(step, 1)
+            c_times_decay(step)
+            c_times_right(step)
+            left_times_deter(step)
+            right_times_x(step)
+            times_tanh(step - 1)
+            add_sides(step)
+            dt_times_b(step + 2)
+            scale_and_store(step - NORM_LAG - 1)
+            mean_stage(step - NORM_LAG)
+            rstd_stage(step - NORM_LAG)
+            finish_softplus(step)

@@ -20,13 +20,12 @@ ROWS = GROUP // P
 N_GROUPS = TOKENS // GROUP
 CH_TILES = CHANNELS // P
 N_BLOCKS = N_GROUPS * CH_TILES
-ROUND = 8
-AHEAD = 2
-NORM_LAG = 5
+ROUNDS = (8, 10, 8, 6)
+AHEAD = 3
+NORM_LAG = 6
 NATURAL_BUFS = 6
 DT_MIN = 1e-4
-EXP_DT_MIN_LESS_1 = DT_MIN + DT_MIN**2 / 2 + DT_MIN**3 / 6
-EXP_CAP = 2.0**60
+SIG_FLOOR = 2.0**-45
 EPS = 1e-4
 
 W_DT, W_B, W_C, W_Z = 0, 1, 2, 3
@@ -51,11 +50,14 @@ def tile_mamba2backbone_pb_t_kernel(
         regroup = stack.enter_context(tc.tile_pool(name="regroup", bufs=3))
         work = stack.enter_context(tc.tile_pool(name="work", bufs=3))
         stats = stack.enter_context(tc.tile_pool(name="stats", bufs=3))
-        dt_pool = stack.enter_context(tc.tile_pool(name="dt_pool", bufs=ROUND + ROUND // 2))
-        gates = stack.enter_context(tc.tile_pool(name="gates", bufs=ROUND + 1))
-        sums = stack.enter_context(tc.tile_pool(name="sums", bufs=CH_TILES + NORM_LAG))
-        psum = stack.enter_context(tc.psum_pool(name="psum", bufs=2))
-        psum_turned = stack.enter_context(tc.psum_pool(name="psum_turned", bufs=4))
+        dt_pool = stack.enter_context(tc.tile_pool(name="dt_pool", bufs=18))
+        decays = stack.enter_context(tc.tile_pool(name="decays", bufs=14))
+        gates = stack.enter_context(tc.tile_pool(name="gates", bufs=10))
+        sums = stack.enter_context(tc.tile_pool(name="sums", bufs=10))
+        psum_acc = stack.enter_context(tc.psum_pool(name="psum_acc", bufs=3))
+        psum_xd = stack.enter_context(tc.psum_pool(name="psum_xd", bufs=2))
+        psum_c = stack.enter_context(tc.psum_pool(name="psum_c", bufs=1))
+        psum_o = stack.enter_context(tc.psum_pool(name="psum_o", bufs=2))
         stack.enter_context(tc.manual_schedule())
 
         vec_rows = keep.tile([P, P], BF16, name="vec_rows", tag="vec_rows")
@@ -64,14 +66,18 @@ def tile_mamba2backbone_pb_t_kernel(
         nc.vector.memset(one_col[:], 1.0)
         neg_half = keep.tile([P, 1], F32, name="neg_half", tag="neg_half")
         nc.vector.memset(neg_half[:], -0.5)
+        floor_col = keep.tile([P, 1], F32, name="floor_col", tag="floor_col")
+        nc.vector.memset(floor_col[:], SIG_FLOOR)
+        eps_col = keep.tile([P, 1], F32, name="eps_col", tag="eps_col")
+        nc.vector.tensor_scalar(out=eps_col[:], in0=one_col[:], scalar1=EPS, scalar2=None, op0=ALU.mult)
         ident_bf = keep.tile([P, P], BF16, name="ident_bf", tag="ident_bf")
         make_identity(nc, ident_bf[:])
         ident_f32 = keep.tile([P, P], F32, name="ident_f32", tag="ident_f32")
         make_identity(nc, ident_f32[:])
-        two_ident = keep.tile([P, P], BF16, name="two_ident", tag="two_ident")
-        nc.vector.tensor_scalar(out=two_ident[:], in0=ident_bf[:], scalar1=2.0, scalar2=None, op0=ALU.mult)
-        exp_dt_min = keep.tile([P, 1], F32, name="exp_dt_min", tag="exp_dt_min")
-        nc.vector.tensor_scalar(out=exp_dt_min[:], in0=one_col[:], scalar1=EXP_DT_MIN_LESS_1, scalar2=None, op0=ALU.add)
+        exp_neg_dt_min = keep.tile([P, 1], F32, name="exp_neg_dt_min", tag="exp_neg_dt_min")
+        nc.vector.tensor_scalar(
+            out=exp_neg_dt_min[:], in0=one_col[:], scalar1=-DT_MIN + DT_MIN**2 / 2 - DT_MIN**3 / 6, scalar2=None, op0=ALU.add
+        )
 
         vectors = (a_base, dt_b, b_b, c_b, z_b, skip)
         for v in range(N_VECTORS):
@@ -112,29 +118,22 @@ def tile_mamba2backbone_pb_t_kernel(
             x_rows[g] = load_x(g)
         gain = keep.tile([P, CHANNELS], BF16, name="gain", tag="gain")
         nc.sync.dma_start(out=gain[:], in_=norm_w.partition_broadcast(P))
-        half_gain = keep.tile([P, CHANNELS], BF16, name="half_gain", tag="half_gain")
 
-        turned_vec = psum_turned.tile([P, P], BF16, name="turned_vec", tag="turned")
+        turned_vec = psum_c.tile([P, P], BF16, name="turned_vec", tag="c")
         nc.tensor.transpose(turned_vec[:], vec_rows[:], ident_bf[:])
         cols = keep.tile([P, N_VECTORS, CH_TILES], F32, name="cols", tag="cols")
         nc.vector.tensor_copy(
             out=cols[:].rearrange("p v t -> p (v t)"), in_=turned_vec[:, : N_VECTORS * CH_TILES]
         )
-        dt_b_min = keep.tile([P, CH_TILES], F32, name="dt_b_min", tag="dt_b_min")
+        neg_cols = keep.tile([P, N_VECTORS, CH_TILES], F32, name="neg_cols", tag="neg_cols")
         nc.vector.tensor_scalar(
-            out=dt_b_min[:], in0=cols[:, V_DT_B, :], scalar1=DT_MIN, scalar2=None, op0=ALU.add
+            out=neg_cols[:].rearrange("p v t -> p (v t)"), in0=turned_vec[:, : N_VECTORS * CH_TILES],
+            scalar1=-1.0, scalar2=None, op0=ALU.mult,
         )
-        half_z_b = keep.tile([P, CH_TILES], F32, name="half_z_b", tag="half_z_b")
+        neg_dt_b_min = keep.tile([P, CH_TILES], F32, name="neg_dt_b_min", tag="neg_dt_b_min")
         nc.vector.tensor_scalar(
-            out=half_z_b[:], in0=cols[:, V_Z_B, :], scalar1=0.5, scalar2=None, op0=ALU.mult
+            out=neg_dt_b_min[:], in0=neg_cols[:, V_DT_B, :], scalar1=-DT_MIN, scalar2=None, op0=ALU.add
         )
-        neg_relu_a = keep.tile([P, CH_TILES], F32, name="neg_relu_a", tag="neg_relu_a")
-        nc.vector.tensor_scalar(
-            out=neg_relu_a[:], in0=cols[:, V_A, :], scalar1=0.0, scalar2=-1.0, op0=ALU.max, op1=ALU.mult
-        )
-        log_a = keep.tile([P, CH_TILES], F32, name="log_a", tag="log_a")
-        nc.scalar.activation(out=log_a[:], in_=cols[:, V_A, :], func=FUNC.Abs)
-        nc.scalar.activation(out=log_a[:], in_=log_a[:], func=FUNC.Exp, scale=-1.0)
 
         x_codes = keep.tile([P, N_GROUPS, GROUP], U32, name="x_codes", tag="x_codes", align_bytes=64)
         x_scales = keep.tile([P, N_GROUPS, GROUP], U8, name="x_scales", tag="x_scales", align_bytes=64)
@@ -146,7 +145,7 @@ def tile_mamba2backbone_pb_t_kernel(
             grouped = regroup.tile([P, ROWS * P * PACK], BF16, name="grouped", tag="grouped", align_bytes=64)
             grouped_words = grouped[:].bitcast(F32).rearrange("p (n u) -> p n u", u=2)
             for half in range(2):
-                turned = psum_turned.tile([P, 2, 2 * P], F32, name="turned", tag="turned")
+                turned = psum_xd.tile([P, 2, 2 * P], F32, name="turned", tag="turned_xd")
                 for u in range(2):
                     for j in range(2):
                         nc.tensor.transpose(
@@ -195,63 +194,77 @@ def tile_mamba2backbone_pb_t_kernel(
             )
             return acc
 
-        dt = {}
+        neg_dt = {}
         decay = {}
-        b_gate = {}
-        z_tanh = {}
+        neg_b = {}
+        z_gate = {}
         c_acc = {}
         turned_xd = {}
         left = {}
         right = {}
-        both = {}
         gated = {}
 
-        def exp_stage(i):
+        def sig_stage(i):
             if is_block(i):
-                acc = project(W_DT, i, psum, "for_scalar")
-                dt[i] = dt_pool.tile([P, GROUP], F32, name="dt", tag="dt")
+                t = i % CH_TILES
+                acc = project(W_DT, i, psum_acc, "acc")
+                neg_dt[i] = dt_pool.tile([P, GROUP], F32, name="neg_dt", tag="neg_dt")
                 nc.scalar.activation(
-                    out=dt[i][:], in_=acc[:], func=FUNC.Exp, bias=cols[:, V_DT_B, i % CH_TILES : i % CH_TILES + 1]
+                    out=neg_dt[i][:], in_=acc[:], func=FUNC.Sigmoid, bias=neg_cols[:, V_DT_B, t : t + 1]
                 )
-
-        def clamp_stage(i):
-            if is_block(i):
-                nc.vector.tensor_scalar(out=dt[i][:], in0=dt[i][:], scalar1=EXP_CAP, scalar2=None, op0=ALU.min)
 
         def ln_stage(i):
             if is_block(i):
-                nc.scalar.activation(out=dt[i][:], in_=dt[i][:], func=FUNC.Ln, scale=exp_dt_min[:], bias=exp_dt_min[:])
+                nc.scalar.activation(
+                    out=neg_dt[i][:], in_=neg_dt[i][:], func=FUNC.Ln, scale=exp_neg_dt_min[:], bias=floor_col[:]
+                )
 
         def large_stage(i):
             if is_block(i):
                 t = i % CH_TILES
-                acc = project(W_DT, i, psum, "for_scalar")
+                acc = project(W_DT, i, psum_acc, "acc")
                 nc.vector.scalar_tensor_tensor(
-                    out=dt[i][:], in0=acc[:], scalar=dt_b_min[:, t : t + 1], in1=dt[i][:], op0=ALU.add, op1=ALU.max
+                    out=neg_dt[i][:], in0=acc[:], scalar=neg_dt_b_min[:, t : t + 1], in1=neg_dt[i][:],
+                    op0=ALU.add, op1=ALU.min,
                 )
 
-        def gate_stage(i):
+        def decay_stage(i):
             if is_block(i):
                 t = i % CH_TILES
-                acc_b = project(W_B, i, psum, "for_scalar")
-                acc_z = project(W_Z, i, psum, "for_scalar")
-                decay[i] = gates.tile([P, GROUP], F32, name="decay", tag="decay")
+                decay[i] = decays.tile([P, GROUP], F32, name="decay", tag="decay")
                 nc.scalar.activation(
-                    out=decay[i][:], in_=dt[i][:], func=FUNC.Exp, scale=a_col[:, t : t + 1]
-                )
-                b_gate[i] = gates.tile([P, GROUP], F32, name="b_gate", tag="b_gate")
-                nc.scalar.activation(out=b_gate[i][:], in_=acc_b[:], func=FUNC.Tanh, bias=cols[:, V_B_B, t : t + 1])
-                z_tanh[i] = gates.tile([P, GROUP], F32, name="z_tanh", tag="z_tanh")
-                nc.scalar.activation(
-                    out=z_tanh[i][:], in_=acc_z[:], func=FUNC.Tanh, scale=0.5, bias=half_z_b[:, t : t + 1]
+                    out=decay[i][:], in_=neg_dt[i][:], func=FUNC.Exp, scale=softplus_a[:, t : t + 1]
                 )
 
-        def feed_stage(i):
+        def b_stage(i):
+            if is_block(i):
+                t = i % CH_TILES
+                acc_b = project(W_B, i, psum_acc, "acc")
+                neg_b[i] = gates.tile([P, GROUP], F32, name="neg_b", tag="neg_b")
+                nc.scalar.activation(
+                    out=neg_b[i][:], in_=acc_b[:], func=FUNC.Tanh, scale=-1.0, bias=neg_cols[:, V_B_B, t : t + 1]
+                )
+
+        def z_stage(i):
+            if is_block(i):
+                t = i % CH_TILES
+                acc_z = project(W_Z, i, psum_acc, "acc")
+                z_gate[i] = gates.tile([P, GROUP], F32, name="z_gate", tag="z_gate")
+                nc.scalar.activation(
+                    out=z_gate[i][:], in_=acc_z[:], func=FUNC.Sigmoid, bias=cols[:, V_Z_B, t : t + 1]
+                )
+
+        def feed_c(i):
+            if is_block(i):
+                c_acc[i] = project(W_C, i, psum_c, "c")
+
+        def feed_xd(i, side):
             if is_block(i):
                 g, t = divmod(i, CH_TILES)
-                c_acc[i] = project(W_C, i, psum_turned, "turned")
-                turned_xd[i] = psum.tile([P, 2, GROUP], BF16, name="turned_xd", tag="turned_xd")
-                for side, rows in enumerate((x_rows[g], deter_rows[g])):
+                if side == 1:
+                    turned_xd[i] = psum_xd.tile([P, 2, GROUP], BF16, name="turned_xd", tag="turned_xd")
+                rows = (x_rows[g], deter_rows[g])[side]
+                if is_block(i):
                     for r in range(ROWS):
                         nc.tensor.transpose(
                             turned_xd[i][:, side, r * P : (r + 1) * P], rows[:, r, t * P : (t + 1) * P], ident_bf[:]
@@ -259,13 +272,13 @@ def tile_mamba2backbone_pb_t_kernel(
 
         def dt_times_b(i):
             if is_block(i):
-                right[i] = work.tile([P, GROUP], F32, name="right", tag="right")
-                nc.gpsimd.tensor_tensor(out=right[i][:], in0=dt[i][:], in1=b_gate[i][:], op=ALU.mult)
+                right[i] = neg_b[i]
+                nc.gpsimd.tensor_tensor(out=right[i][:], in0=neg_dt[i][:], in1=neg_b[i][:], op=ALU.mult)
 
         def c_times_decay(i):
             if is_block(i):
                 t = i % CH_TILES
-                left[i] = work.tile([P, GROUP], F32, name="left", tag="left")
+                left[i] = sums.tile([P, GROUP], F32, name="left", tag="left")
                 nc.vector.scalar_tensor_tensor(
                     out=left[i][:], in0=c_acc[i][:], scalar=cols[:, V_C_B, t : t + 1], in1=decay[i][:],
                     op0=ALU.add, op1=ALU.mult,
@@ -293,17 +306,18 @@ def tile_mamba2backbone_pb_t_kernel(
                     op0=ALU.add, op1=ALU.mult,
                 )
 
+        def on_vector(i):
+            return False
+
         def add_sides(i):
             if is_block(i):
-                both[i] = work.tile([P, GROUP], F32, name="both", tag="both")
-                nc.gpsimd.tensor_tensor(out=both[i][:], in0=left[i][:], in1=right[i][:], op=ALU.add)
+                engine = nc.vector if on_vector(i) else nc.gpsimd
+                engine.tensor_tensor(out=left[i][:], in0=left[i][:], in1=right[i][:], op=ALU.add)
 
-        def times_tanh(i):
+        def times_z(i):
             if is_block(i):
-                gated[i] = sums.tile([P, GROUP], F32, name="gated", tag="gated")
-                nc.vector.scalar_tensor_tensor(
-                    out=gated[i][:], in0=z_tanh[i][:], scalar=1.0, in1=both[i][:], op0=ALU.add, op1=ALU.mult
-                )
+                gated[i] = left[i]
+                nc.gpsimd.tensor_tensor(out=gated[i][:], in0=left[i][:], in1=z_gate[i][:], op=ALU.mult)
 
         o_turned = {}
         sum_sq = {}
@@ -313,9 +327,9 @@ def tile_mamba2backbone_pb_t_kernel(
         def turn_back(n):
             if is_block(n):
                 g, r = divmod(n, ROWS)
-                o_turned[n] = psum_turned.tile([P, CHANNELS], F32, name="turned", tag="turned")
+                o_turned[n] = psum_o.tile([P, CHANNELS], F32, name="o_turned", tag="o_turned")
                 nc.tensor.matmul(
-                    out=o_turned[n][:], lhsT=two_ident[:], rhs=deter_rows[g][:, r, :], start=True, stop=False
+                    out=o_turned[n][:], lhsT=ident_bf[:], rhs=deter_rows[g][:, r, :], start=True, stop=False
                 )
                 for t in range(CH_TILES):
                     nc.tensor.matmul(
@@ -326,17 +340,20 @@ def tile_mamba2backbone_pb_t_kernel(
                         start=False,
                         stop=(t == CH_TILES - 1),
                     )
+                if r == ROWS - 1:
+                    load_deter(g + NATURAL_BUFS)
+
+        def square_stage(n):
+            if is_block(n):
                 squares = work.tile([P, CHANNELS], BF16, name="squares", tag="squares")
                 sum_sq[n] = stats.tile([P, 1], F32, name="sum_sq", tag="sum_sq")
                 nc.scalar.activation(out=squares[:], in_=o_turned[n][:], func=FUNC.Square, accum_out=sum_sq[n][:])
-                if r == ROWS - 1:
-                    load_deter(g + NATURAL_BUFS)
 
         def mean_stage(n):
             if is_block(n):
                 mean_sq[n] = stats.tile([P, 1], F32, name="mean_sq", tag="mean_sq")
-                nc.vector.tensor_scalar(
-                    out=mean_sq[n][:], in0=sum_sq[n][:], scalar1=0.25 / CHANNELS, scalar2=EPS, op0=ALU.mult, op1=ALU.add
+                nc.scalar.activation(
+                    out=mean_sq[n][:], in_=sum_sq[n][:], func=FUNC.Identity, scale=1.0 / CHANNELS, bias=eps_col[:]
                 )
 
         def rstd_stage(n):
@@ -349,72 +366,107 @@ def tile_mamba2backbone_pb_t_kernel(
                 g, r = divmod(n, ROWS)
                 result = work.tile([P, CHANNELS], F32, name="result", tag="result")
                 nc.vector.scalar_tensor_tensor(
-                    out=result[:], in0=o_turned[n][:], scalar=rstd[n][:], in1=half_gain[:], op0=ALU.mult, op1=ALU.mult
+                    out=result[:], in0=o_turned[n][:], scalar=rstd[n][:], in1=gain[:], op0=ALU.mult, op1=ALU.mult
                 )
                 nc.sync.dma_start(out=out_groups[g, :, r, :], in_=result[:])
 
+        nc.vector.tensor_scalar(out=w_rows[W_DT][:], in0=w_rows[W_DT][:], scalar1=-1.0, scalar2=None, op0=ALU.mult)
+        log_a = keep.tile([P, CH_TILES], F32, name="log_a", tag="log_a")
+        nc.scalar.activation(out=log_a[:], in_=cols[:, V_A, :], func=FUNC.Sigmoid, scale=-1.0)
+        first = ROUNDS[0]
         quantise_all([weight_job(W_DT), x_job(0)])
-        exp_stage(0)
-        exp_stage(1)
-        quantise_all([x_job(1)])
-        for i in range(2, ROUND):
-            exp_stage(i)
-        quantise_all([weight_job(W_B)])
-        for i in range(ROUND // 2):
-            clamp_stage(i)
-        quantise_all([weight_job(W_Z)])
-        for i in range(ROUND // 2, ROUND):
-            clamp_stage(i)
-        nc.scalar.activation(out=log_a[:], in_=log_a[:], func=FUNC.Ln, bias=one_col[:])
-        a_col = keep.tile([P, CH_TILES], F32, name="a_col", tag="a_col")
-        nc.gpsimd.tensor_tensor(out=a_col[:], in0=neg_relu_a[:], in1=log_a[:], op=ALU.subtract)
-        for i in range(ROUND):
+        for i in range(min(first, CH_TILES)):
+            sig_stage(i)
+        quantise_all([x_job(g) for g in range(1, (first + CH_TILES - 1) // CH_TILES)] + [weight_job(W_B), weight_job(W_Z)])
+        for i in range(CH_TILES, first):
+            sig_stage(i)
+        for i in range(AHEAD):
+            b_stage(i)
+            z_stage(i)
+        nc.scalar.activation(out=log_a[:], in_=log_a[:], func=FUNC.Ln, bias=floor_col[:])
+        softplus_a = keep.tile([P, CH_TILES], F32, name="softplus_a", tag="softplus_a")
+        nc.vector.scalar_tensor_tensor(
+            out=softplus_a[:], in0=log_a[:], scalar=-1.0, in1=cols[:, V_A, :], op0=ALU.mult, op1=ALU.max
+        )
+        for i in range(first):
             ln_stage(i)
         quantise_all([weight_job(W_C)])
-        for i in range(ROUND // 2):
+        for i in range(first):
             large_stage(i)
-        quantise_all([x_job(2)])
-        for i in range(ROUND // 2, ROUND):
-            large_stage(i)
-        quantise_all([x_job(g) for g in range(3, N_GROUPS)])
+        for i in range(first):
+            decay_stage(i)
+        quantise_all([x_job(g) for g in range((first + CH_TILES - 1) // CH_TILES, 8)])
         for g in range(2, NATURAL_BUFS):
             load_deter(g)
-        nc.vector.tensor_scalar(out=half_gain[:], in0=gain[:], scalar1=0.5, scalar2=None, op0=ALU.mult)
 
-        def scalar_stage(step, half):
-            this_round, s = divmod(step + AHEAD, ROUND)
-            if s < ROUND // 2:
-                gate_stage(ROUND * this_round + 2 * s + half)
-            else:
-                for j in range(2):
-                    i = ROUND * (this_round + 1) + (ROUND // 2) * (s % 2) + 2 * half + j
-                    if s < ROUND // 2 + 2:
-                        exp_stage(i)
-                    else:
-                        ln_stage(i)
+        def part(tasks, n, j):
+            return tasks[len(tasks) * j // n : len(tasks) * (j + 1) // n]
 
-        def finish_softplus(step):
-            this_round, s = divmod(step + AHEAD, ROUND)
-            for j in range(ROUND // 2):
-                i = ROUND * (this_round + 1) + (ROUND // 2) * (s % 2) + j
-                if ROUND // 2 <= s < ROUND // 2 + 2:
-                    clamp_stage(i)
-                elif s >= ROUND // 2 + 2:
-                    large_stage(i)
+        plan = {}
+        large_plan = {}
+        start = 0
+        for k in range(len(ROUNDS)):
+            n = ROUNDS[k]
+            m = ROUNDS[k + 1] if k + 1 < len(ROUNDS) else 0
+            nxt = [start + n + i for i in range(m)]
+            burst = max(2, int(n * 0.45 + 0.5)) if m else 0
+            calm = n - burst
+            ln_steps = (burst + 1) // 2
+            for s in range(n):
+                tasks = []
+                if s < calm:
+                    for i in part([start + AHEAD + i for i in range(n)], calm, s):
+                        tasks.append((b_stage, i))
+                        tasks.append((z_stage, i))
+                    for i in part(nxt, calm, s):
+                        tasks.append((sig_stage, i))
+                elif s < calm + ln_steps:
+                    for i in part(nxt, ln_steps, s - calm):
+                        tasks.append((ln_stage, i))
+                        large_plan.setdefault(start + s, []).append(i)
+                else:
+                    for i in part(nxt, burst - ln_steps, s - calm - ln_steps):
+                        tasks.append((decay_stage, i))
+                plan[start + s] = tasks
+            start += n
 
-        for step in range(-AHEAD, N_BLOCKS + NORM_LAG + 2):
-            feed_stage(step + 1)
-            scalar_stage(step, 0)
+        dt_times_b(0)
+        dt_times_b(1)
+        feed_c(0)
+        feed_xd(0, 1)
+        feed_xd(0, 0)
+        for step in range(N_BLOCKS + NORM_LAG + 3):
+            tasks = plan.get(step, [])
+            pieces = [part(tasks, 5, j) for j in range(5)]
+            for f, i in pieces[0]:
+                f(i)
+            feed_xd(step + 1, 1)
+            for f, i in pieces[1]:
+                f(i)
             turn_back(step - NORM_LAG)
-            scalar_stage(step, 1)
+            mean_stage(step - NORM_LAG - 1)
+            for f, i in pieces[2]:
+                f(i)
+            feed_xd(step + 1, 0)
+            for f, i in pieces[3]:
+                f(i)
+            square_stage(step - NORM_LAG)
+            for f, i in pieces[4]:
+                f(i)
             c_times_decay(step)
+            rstd_stage(step - NORM_LAG - 1)
+            if is_block(step - 1) and on_vector(step - 1):
+                add_sides(step - 1)
             c_times_right(step)
+            feed_c(step + 1)
             left_times_deter(step)
             right_times_x(step)
-            times_tanh(step - 1)
-            add_sides(step)
-            dt_times_b(step + 2)
             scale_and_store(step - NORM_LAG - 1)
-            mean_stage(step - NORM_LAG)
-            rstd_stage(step - NORM_LAG)
-            finish_softplus(step)
+            if is_block(step - 1) and on_vector(step - 1):
+                times_z(step - 1)
+            dt_times_b(step + 2)
+            if is_block(step) and not on_vector(step):
+                add_sides(step)
+                times_z(step)
+            for i in large_plan.get(step, []):
+                large_stage(i)

@@ -58,7 +58,7 @@ def tile_mamba2backbone_pb_t_kernel(
         psum_xd = stack.enter_context(tc.psum_pool(name="psum_xd", bufs=2))
         psum_c = stack.enter_context(tc.psum_pool(name="psum_c", bufs=1))
         psum_o = stack.enter_context(tc.psum_pool(name="psum_o", bufs=2))
-        stack.enter_context(tc.manual_schedule())
+        stack.enter_context(tc.manual_schedule(engines={mybir.EngineType.Activation}))
 
         vec_rows = keep.tile([P, P], BF16, name="vec_rows", tag="vec_rows")
         nc.vector.memset(vec_rows[:], 0.0)
@@ -307,7 +307,7 @@ def tile_mamba2backbone_pb_t_kernel(
                 )
 
         def on_vector(i):
-            return False
+            return True
 
         def add_sides(i):
             if is_block(i):

from contextlib import ExitStack

import concourse.mybir as mybir
from concourse.masks import make_identity

F32 = mybir.dt.float32
BF16 = mybir.dt.bfloat16
U32 = mybir.dt.uint32
U8 = mybir.dt.uint8
FP8X4 = mybir.dt.float8_e4m3fn_x4
FUNC = mybir.ActivationFunctionType
ALU = mybir.AluOpType

P = 128
PACK = 4
TOKENS = 4096
CHANNELS = 512
GROUP = 512
ROWS = GROUP // P
N_GROUPS = TOKENS // GROUP
CH_TILES = CHANNELS // P
N_BLOCKS = N_GROUPS * CH_TILES
ROUNDS = (8, 10, 8, 6)
AHEAD = 3
NORM_LAG = 6
NATURAL_BUFS = 6
DT_MIN = 1e-4
SIG_FLOOR = 2.0**-45
EPS = 1e-4

W_DT, W_B, W_C, W_Z = 0, 1, 2, 3
N_WEIGHTS = 4
V_A, V_DT_B, V_B_B, V_C_B, V_Z_B, V_SKIP = 0, 1, 2, 3, 4, 5
N_VECTORS = 6

FLOPS = 4 * 2 * TOKENS * CHANNELS * CHANNELS


def tile_mamba2backbone_pb_t_kernel(
    tc, x, deter, a_base, dt_w, dt_b, b_w, b_b, c_w, c_b, z_w, z_b, skip, norm_w, out
):
    nc = tc.nc
    x_groups = x.rearrange("(g p r) c -> g p r c", p=P, r=ROWS)
    deter_groups = deter.rearrange("(g p r) c -> g p r c", p=P, r=ROWS)
    out_groups = out.rearrange("(g p r) c -> g p r c", p=P, r=ROWS)

    with ExitStack() as stack:
        keep = stack.enter_context(tc.tile_pool(name="keep", bufs=1))
        natural = stack.enter_context(tc.tile_pool(name="natural", bufs=NATURAL_BUFS))
        regroup = stack.enter_context(tc.tile_pool(name="regroup", bufs=3))
        work = stack.enter_context(tc.tile_pool(name="work", bufs=3))
        stats = stack.enter_context(tc.tile_pool(name="stats", bufs=3))
        dt_pool = stack.enter_context(tc.tile_pool(name="dt_pool", bufs=18))
        decays = stack.enter_context(tc.tile_pool(name="decays", bufs=14))
        gates = stack.enter_context(tc.tile_pool(name="gates", bufs=10))
        sums = stack.enter_context(tc.tile_pool(name="sums", bufs=10))
        psum_acc = stack.enter_context(tc.psum_pool(name="psum_acc", bufs=3))
        psum_xd = stack.enter_context(tc.psum_pool(name="psum_xd", bufs=2))
        psum_c = stack.enter_context(tc.psum_pool(name="psum_c", bufs=1))
        psum_o = stack.enter_context(tc.psum_pool(name="psum_o", bufs=2))
        stack.enter_context(tc.manual_schedule(engines={mybir.EngineType.Activation}))

        vec_rows = keep.tile([P, P], BF16, name="vec_rows", tag="vec_rows")
        nc.vector.memset(vec_rows[:], 0.0)
        one_col = keep.tile([P, 1], F32, name="one_col", tag="one_col")
        nc.vector.memset(one_col[:], 1.0)
        neg_half = keep.tile([P, 1], F32, name="neg_half", tag="neg_half")
        nc.vector.memset(neg_half[:], -0.5)
        floor_col = keep.tile([P, 1], F32, name="floor_col", tag="floor_col")
        nc.vector.memset(floor_col[:], SIG_FLOOR)
        eps_col = keep.tile([P, 1], F32, name="eps_col", tag="eps_col")
        nc.vector.tensor_scalar(out=eps_col[:], in0=one_col[:], scalar1=EPS, scalar2=None, op0=ALU.mult)
        ident_bf = keep.tile([P, P], BF16, name="ident_bf", tag="ident_bf")
        make_identity(nc, ident_bf[:])
        ident_f32 = keep.tile([P, P], F32, name="ident_f32", tag="ident_f32")
        make_identity(nc, ident_f32[:])
        exp_neg_dt_min = keep.tile([P, 1], F32, name="exp_neg_dt_min", tag="exp_neg_dt_min")
        nc.vector.tensor_scalar(
            out=exp_neg_dt_min[:], in0=one_col[:], scalar1=-DT_MIN + DT_MIN**2 / 2 - DT_MIN**3 / 6, scalar2=None, op0=ALU.add
        )

        vectors = (a_base, dt_b, b_b, c_b, z_b, skip)
        for v in range(N_VECTORS):
            nc.sync.dma_start(
                out=vec_rows[CH_TILES * v : CH_TILES * (v + 1), :],
                in_=vectors[v].rearrange("(t p) -> t p", p=P),
            )

        def load_weight(w):
            rows = natural.tile([P, ROWS, CHANNELS], BF16, name="rows", tag="rows")
            nc.sync.dma_start(out=rows[:], in_=w.rearrange("(t p) k -> p t k", p=P))
            return rows

        def load_x(g):
            rows = keep.tile([P, ROWS, CHANNELS], BF16, name="x_rows%d" % g, tag="x_rows%d" % g)
            nc.sync.dma_start(out=rows[:], in_=x_groups[g])
            return rows

        def load_deter(g):
            if g < N_GROUPS:
                deter_rows[g] = natural.tile([P, ROWS, CHANNELS], BF16, name="rows", tag="rows")
                nc.sync.dma_start(out=deter_rows[g][:], in_=deter_groups[g])

        x_rows = {}
        deter_rows = {}
        w_rows = {}
        w_rows[W_DT] = load_weight(dt_w)
        x_rows[0] = load_x(0)
        x_rows[1] = load_x(1)
        w_rows[W_B] = load_weight(b_w)
        w_rows[W_Z] = load_weight(z_w)
        w_rows[W_C] = load_weight(c_w)
        x_rows[2] = load_x(2)
        x_rows[3] = load_x(3)
        load_deter(0)
        load_deter(1)
        for g in range(4, N_GROUPS):
            x_rows[g] = load_x(g)
        gain = keep.tile([P, CHANNELS], BF16, name="gain", tag="gain")
        nc.sync.dma_start(out=gain[:], in_=norm_w.partition_broadcast(P))

        turned_vec = psum_c.tile([P, P], BF16, name="turned_vec", tag="c")
        nc.tensor.transpose(turned_vec[:], vec_rows[:], ident_bf[:])
        cols = keep.tile([P, N_VECTORS, CH_TILES], F32, name="cols", tag="cols")
        nc.vector.tensor_copy(
            out=cols[:].rearrange("p v t -> p (v t)"), in_=turned_vec[:, : N_VECTORS * CH_TILES]
        )
        neg_cols = keep.tile([P, N_VECTORS, CH_TILES], F32, name="neg_cols", tag="neg_cols")
        nc.vector.tensor_scalar(
            out=neg_cols[:].rearrange("p v t -> p (v t)"), in0=turned_vec[:, : N_VECTORS * CH_TILES],
            scalar1=-1.0, scalar2=None, op0=ALU.mult,
        )
        neg_dt_b_min = keep.tile([P, CH_TILES], F32, name="neg_dt_b_min", tag="neg_dt_b_min")
        nc.vector.tensor_scalar(
            out=neg_dt_b_min[:], in0=neg_cols[:, V_DT_B, :], scalar1=-DT_MIN, scalar2=None, op0=ALU.add
        )

        x_codes = keep.tile([P, N_GROUPS, GROUP], U32, name="x_codes", tag="x_codes", align_bytes=64)
        x_scales = keep.tile([P, N_GROUPS, GROUP], U8, name="x_scales", tag="x_scales", align_bytes=64)
        w_codes = keep.tile([P, N_WEIGHTS, CHANNELS], U32, name="w_codes", tag="w_codes", align_bytes=64)
        w_scales = keep.tile([P, N_WEIGHTS, CHANNELS], U8, name="w_scales", tag="w_scales", align_bytes=64)

        def turn_rows(rows):
            words = rows[:].bitcast(F32)
            grouped = regroup.tile([P, ROWS * P * PACK], BF16, name="grouped", tag="grouped", align_bytes=64)
            grouped_words = grouped[:].bitcast(F32).rearrange("p (n u) -> p n u", u=2)
            for half in range(2):
                turned = psum_xd.tile([P, 2, 2 * P], F32, name="turned", tag="turned_xd")
                for u in range(2):
                    for j in range(2):
                        nc.tensor.transpose(
                            turned[:, u, j * P : (j + 1) * P],
                            words[:, 2 * half + j, u * P : (u + 1) * P],
                            ident_f32[:],
                        )
                nc.vector.tensor_copy(
                    out=grouped_words[:, half * 2 * P : (half + 1) * 2 * P, :],
                    in_=turned[:].rearrange("p u n -> p n u"),
                )
            return grouped

        def quantise(grouped, codes, scales):
            nc.vector.quantize_mx(out=codes.bitcast(FP8X4), scales=scales, in_=grouped[:])

        def quantise_all(jobs):
            waiting = None
            for rows, codes, scales in jobs:
                grouped = turn_rows(rows)
                if waiting is not None:
                    quantise(*waiting)
                waiting = (grouped, codes, scales)
            quantise(*waiting)

        def weight_job(w):
            return (w_rows[w], w_codes[:, w, :], w_scales[:, w, :])

        def x_job(g):
            return (x_rows[g], x_codes[:, g, :], x_scales[:, g, :])

        def is_block(i):
            return 0 <= i < N_BLOCKS

        def project(w, i, pool, tag):
            g, t = divmod(i, CH_TILES)
            acc = pool.tile([P, GROUP], F32, name=tag, tag=tag)
            nc.tensor.matmul_mx(
                out=acc[:],
                lhsT=w_codes[:, w, t * P : (t + 1) * P].bitcast(FP8X4),
                lhsT_scale=w_scales[:, w, t * P : (t + 1) * P],
                rhs=x_codes[:, g, :].bitcast(FP8X4),
                rhs_scale=x_scales[:, g, :],
                start=True,
                stop=True,
            )
            return acc

        neg_dt = {}
        decay = {}
        neg_b = {}
        z_gate = {}
        c_acc = {}
        turned_xd = {}
        left = {}
        right = {}
        gated = {}

        def sig_stage(i):
            if is_block(i):
                t = i % CH_TILES
                acc = project(W_DT, i, psum_acc, "acc")
                neg_dt[i] = dt_pool.tile([P, GROUP], F32, name="neg_dt", tag="neg_dt")
                nc.scalar.activation(
                    out=neg_dt[i][:], in_=acc[:], func=FUNC.Sigmoid, bias=neg_cols[:, V_DT_B, t : t + 1]
                )

        def ln_stage(i):
            if is_block(i):
                nc.scalar.activation(
                    out=neg_dt[i][:], in_=neg_dt[i][:], func=FUNC.Ln, scale=exp_neg_dt_min[:], bias=floor_col[:]
                )

        def large_stage(i):
            if is_block(i):
                t = i % CH_TILES
                acc = project(W_DT, i, psum_acc, "acc")
                nc.vector.scalar_tensor_tensor(
                    out=neg_dt[i][:], in0=acc[:], scalar=neg_dt_b_min[:, t : t + 1], in1=neg_dt[i][:],
                    op0=ALU.add, op1=ALU.min,
                )

        def decay_stage(i):
            if is_block(i):
                t = i % CH_TILES
                decay[i] = decays.tile([P, GROUP], F32, name="decay", tag="decay")
                nc.scalar.activation(
                    out=decay[i][:], in_=neg_dt[i][:], func=FUNC.Exp, scale=softplus_a[:, t : t + 1]
                )

        def b_stage(i):
            if is_block(i):
                t = i % CH_TILES
                acc_b = project(W_B, i, psum_acc, "acc")
                neg_b[i] = gates.tile([P, GROUP], F32, name="neg_b", tag="neg_b")
                nc.scalar.activation(
                    out=neg_b[i][:], in_=acc_b[:], func=FUNC.Tanh, scale=-1.0, bias=neg_cols[:, V_B_B, t : t + 1]
                )

        def z_stage(i):
            if is_block(i):
                t = i % CH_TILES
                acc_z = project(W_Z, i, psum_acc, "acc")
                z_gate[i] = gates.tile([P, GROUP], F32, name="z_gate", tag="z_gate")
                nc.scalar.activation(
                    out=z_gate[i][:], in_=acc_z[:], func=FUNC.Sigmoid, bias=cols[:, V_Z_B, t : t + 1]
                )

        def feed_c(i):
            if is_block(i):
                c_acc[i] = project(W_C, i, psum_c, "c")

        def feed_xd(i, side):
            if is_block(i):
                g, t = divmod(i, CH_TILES)
                if side == 1:
                    turned_xd[i] = psum_xd.tile([P, 2, GROUP], BF16, name="turned_xd", tag="turned_xd")
                rows = (x_rows[g], deter_rows[g])[side]
                if is_block(i):
                    for r in range(ROWS):
                        nc.tensor.transpose(
                            turned_xd[i][:, side, r * P : (r + 1) * P], rows[:, r, t * P : (t + 1) * P], ident_bf[:]
                        )

        def dt_times_b(i):
            if is_block(i):
                right[i] = neg_b[i]
                nc.gpsimd.tensor_tensor(out=right[i][:], in0=neg_dt[i][:], in1=neg_b[i][:], op=ALU.mult)

        def c_times_decay(i):
            if is_block(i):
                t = i % CH_TILES
                left[i] = sums.tile([P, GROUP], F32, name="left", tag="left")
                nc.vector.scalar_tensor_tensor(
                    out=left[i][:], in0=c_acc[i][:], scalar=cols[:, V_C_B, t : t + 1], in1=decay[i][:],
                    op0=ALU.add, op1=ALU.mult,
                )

        def c_times_right(i):
            if is_block(i):
                t = i % CH_TILES
                nc.vector.scalar_tensor_tensor(
                    out=right[i][:], in0=c_acc[i][:], scalar=cols[:, V_C_B, t : t + 1], in1=right[i][:],
                    op0=ALU.add, op1=ALU.mult,
                )

        def left_times_deter(i):
            if is_block(i):
                nc.vector.scalar_tensor_tensor(
                    out=left[i][:], in0=left[i][:], scalar=-1.0, in1=turned_xd[i][:, 1, :], op0=ALU.add, op1=ALU.mult
                )

        def right_times_x(i):
            if is_block(i):
                t = i % CH_TILES
                nc.vector.scalar_tensor_tensor(
                    out=right[i][:], in0=right[i][:], scalar=cols[:, V_SKIP, t : t + 1], in1=turned_xd[i][:, 0, :],
                    op0=ALU.add, op1=ALU.mult,
                )

        def on_vector(i):
            return True

        def add_sides(i):
            if is_block(i):
                engine = nc.vector if on_vector(i) else nc.gpsimd
                engine.tensor_tensor(out=left[i][:], in0=left[i][:], in1=right[i][:], op=ALU.add)

        def times_z(i):
            if is_block(i):
                gated[i] = left[i]
                nc.gpsimd.tensor_tensor(out=gated[i][:], in0=left[i][:], in1=z_gate[i][:], op=ALU.mult)

        o_turned = {}
        sum_sq = {}
        mean_sq = {}
        rstd = {}

        def turn_back(n):
            if is_block(n):
                g, r = divmod(n, ROWS)
                o_turned[n] = psum_o.tile([P, CHANNELS], F32, name="o_turned", tag="o_turned")
                nc.tensor.matmul(
                    out=o_turned[n][:], lhsT=ident_bf[:], rhs=deter_rows[g][:, r, :], start=True, stop=False
                )
                for t in range(CH_TILES):
                    nc.tensor.matmul(
                        out=o_turned[n][:, t * P : (t + 1) * P],
                        lhsT=gated[CH_TILES * g + t][:, r * P : (r + 1) * P],
                        rhs=ident_f32[:],
                        is_transpose=True,
                        start=False,
                        stop=(t == CH_TILES - 1),
                    )
                if r == ROWS - 1:
                    load_deter(g + NATURAL_BUFS)

        def square_stage(n):
            if is_block(n):
                squares = work.tile([P, CHANNELS], BF16, name="squares", tag="squares")
                sum_sq[n] = stats.tile([P, 1], F32, name="sum_sq", tag="sum_sq")
                nc.scalar.activation(out=squares[:], in_=o_turned[n][:], func=FUNC.Square, accum_out=sum_sq[n][:])

        def mean_stage(n):
            if is_block(n):
                mean_sq[n] = stats.tile([P, 1], F32, name="mean_sq", tag="mean_sq")
                nc.scalar.activation(
                    out=mean_sq[n][:], in_=sum_sq[n][:], func=FUNC.Identity, scale=1.0 / CHANNELS, bias=eps_col[:]
                )

        def rstd_stage(n):
            if is_block(n):
                rstd[n] = stats.tile([P, 1], F32, name="rstd", tag="rstd")
                nc.gpsimd.tensor_tensor(out=rstd[n][:], in0=mean_sq[n][:], in1=neg_half[:], op=ALU.pow)

        def scale_and_store(n):
            if is_block(n):
                g, r = divmod(n, ROWS)
                result = work.tile([P, CHANNELS], F32, name="result", tag="result")
                nc.vector.scalar_tensor_tensor(
                    out=result[:], in0=o_turned[n][:], scalar=rstd[n][:], in1=gain[:], op0=ALU.mult, op1=ALU.mult
                )
                nc.sync.dma_start(out=out_groups[g, :, r, :], in_=result[:])

        nc.vector.tensor_scalar(out=w_rows[W_DT][:], in0=w_rows[W_DT][:], scalar1=-1.0, scalar2=None, op0=ALU.mult)
        log_a = keep.tile([P, CH_TILES], F32, name="log_a", tag="log_a")
        nc.scalar.activation(out=log_a[:], in_=cols[:, V_A, :], func=FUNC.Sigmoid, scale=-1.0)
        first = ROUNDS[0]
        quantise_all([weight_job(W_DT), x_job(0)])
        for i in range(min(first, CH_TILES)):
            sig_stage(i)
        quantise_all([x_job(g) for g in range(1, (first + CH_TILES - 1) // CH_TILES)] + [weight_job(W_B), weight_job(W_Z)])
        for i in range(CH_TILES, first):
            sig_stage(i)
        for i in range(AHEAD):
            b_stage(i)
            z_stage(i)
        nc.scalar.activation(out=log_a[:], in_=log_a[:], func=FUNC.Ln, bias=floor_col[:])
        softplus_a = keep.tile([P, CH_TILES], F32, name="softplus_a", tag="softplus_a")
        nc.vector.scalar_tensor_tensor(
            out=softplus_a[:], in0=log_a[:], scalar=-1.0, in1=cols[:, V_A, :], op0=ALU.mult, op1=ALU.max
        )
        for i in range(first):
            ln_stage(i)
        quantise_all([weight_job(W_C)])
        for i in range(first):
            large_stage(i)
        for i in range(first):
            decay_stage(i)
        quantise_all([x_job(g) for g in range((first + CH_TILES - 1) // CH_TILES, 8)])
        for g in range(2, NATURAL_BUFS):
            load_deter(g)

        def part(tasks, n, j):
            return tasks[len(tasks) * j // n : len(tasks) * (j + 1) // n]

        plan = {}
        large_plan = {}
        start = 0
        for k in range(len(ROUNDS)):
            n = ROUNDS[k]
            m = ROUNDS[k + 1] if k + 1 < len(ROUNDS) else 0
            nxt = [start + n + i for i in range(m)]
            burst = max(2, int(n * 0.45 + 0.5)) if m else 0
            calm = n - burst
            ln_steps = (burst + 1) // 2
            for s in range(n):
                tasks = []
                if s < calm:
                    for i in part([start + AHEAD + i for i in range(n)], calm, s):
                        tasks.append((b_stage, i))
                        tasks.append((z_stage, i))
                    for i in part(nxt, calm, s):
                        tasks.append((sig_stage, i))
                elif s < calm + ln_steps:
                    for i in part(nxt, ln_steps, s - calm):
                        tasks.append((ln_stage, i))
                        large_plan.setdefault(start + s, []).append(i)
                else:
                    for i in part(nxt, burst - ln_steps, s - calm - ln_steps):
                        tasks.append((decay_stage, i))
                plan[start + s] = tasks
            start += n

        dt_times_b(0)
        dt_times_b(1)
        feed_c(0)
        feed_xd(0, 1)
        feed_xd(0, 0)
        for step in range(N_BLOCKS + NORM_LAG + 3):
            tasks = plan.get(step, [])
            pieces = [part(tasks, 5, j) for j in range(5)]
            for f, i in pieces[0]:
                f(i)
            feed_xd(step + 1, 1)
            for f, i in pieces[1]:
                f(i)
            turn_back(step - NORM_LAG)
            mean_stage(step - NORM_LAG - 1)
            for f, i in pieces[2]:
                f(i)
            feed_xd(step + 1, 0)
            for f, i in pieces[3]:
                f(i)
            square_stage(step - NORM_LAG)
            for f, i in pieces[4]:
                f(i)
            c_times_decay(step)
            rstd_stage(step - NORM_LAG - 1)
            if is_block(step - 1) and on_vector(step - 1):
                add_sides(step - 1)
            c_times_right(step)
            feed_c(step + 1)
            left_times_deter(step)
            right_times_x(step)
            scale_and_store(step - NORM_LAG - 1)
            if is_block(step - 1) and on_vector(step - 1):
                times_z(step - 1)
            dt_times_b(step + 2)
            if is_block(step) and not on_vector(step):
                add_sides(step)
                times_z(step)
            for i in large_plan.get(step, []):
                large_stage(i)
